import numpy as np
import ml_dtypes


def mxq(x, axis, fmt="e4m3"):
    dtype, down = {"e4m3": (ml_dtypes.float8_e4m3fn, 7), "e5m2": (ml_dtypes.float8_e5m2, 14)}[fmt]
    v = np.moveaxis(np.asarray(x, np.float32).astype(ml_dtypes.bfloat16).astype(np.float64), axis, -1)
    blocks = v.reshape(v.shape[:-1] + (-1, 32))
    amax = np.abs(blocks).max(-1, keepdims=True)
    byte = np.maximum(np.where(amax > 0, np.frexp(amax)[1] - 1 + 127, 0) - down, 1)
    scale = np.exp2(byte - 127.0)
    codes = (blocks / scale).astype(np.float32).astype(dtype).astype(np.float64)
    return np.moveaxis((codes * scale).reshape(v.shape), -1, axis)


WIDE = False


def mx_kscale(k):
    if not WIDE:
        return np.ones(k)
    levels = np.array([10, -10, 5, -5, 0])
    a = np.random.permutation(np.resize(levels, k // 512 * 4)).reshape(k // 512, 4)
    idx = np.arange(k)
    return np.exp2(a[idx // 512, idx % 128 // 32])


BF16 = ml_dtypes.bfloat16


def bf(x):
    return np.asarray(x, np.float32).astype(BF16)


def f64(x):
    return np.asarray(x).astype(np.float64)


B, D, ELL = 4096, 512, 4


def setup_inputs():
    s, t = mx_kscale(D), mx_kscale(D)
    return {"x": bf(np.random.standard_normal((B, D))),
            "phi_j": bf(np.random.standard_normal((B, D)) * 0.7 * t / s),
            "phi_k": bf(np.random.standard_normal((B, D)) * 0.7 * s),
            "w_i": bf(np.random.standard_normal((D, D)) / np.sqrt(D) / t),
            "w_j": bf(np.random.standard_normal((D, D)) / np.sqrt(D) * t[:, None] / s)}


def reference(x, phi_j, phi_k, w_i, w_j):
    x, phi_j, phi_k = f64(x), f64(phi_j), f64(phi_k)
    th = np.tanh(x)
    d1 = 1.0 - th * th
    d2 = -2.0 * th * d1
    jvp_jk = mxq(d1 * phi_k, 1, "e4m3") @ mxq(f64(w_j), 1, "e4m3").T
    u = d2 * phi_k * phi_j + d1 * jvp_jk
    return mxq(u, 1, "e4m3") @ mxq(f64(w_i), 1, "e4m3").T

@@ -1,0 +1,303 @@
+from contextlib import ExitStack
+
+import concourse.mybir as mybir
+from concourse.masks import make_identity
+
+F32 = mybir.dt.float32
+BF16 = mybir.dt.bfloat16
+U32 = mybir.dt.uint32
+U8 = mybir.dt.uint8
+FP8X4 = mybir.dt.float8_e4m3fn_x4
+ACT = mybir.ActivationFunctionType
+ALU = mybir.AluOpType
+
+P = 128
+B = 4096
+D = 512
+SLOTS = 4
+WORDS = D // 2
+N_BLOCKS = B // P
+STEP_BLOCKS = 2
+N_STEPS = N_BLOCKS // STEP_BLOCKS
+STEP_COLS = STEP_BLOCKS * P
+STEP_ELEMS = STEP_COLS * SLOTS
+BLOCK_ELEMS = P * SLOTS
+LOAD_AHEAD = 4
+LAG_G = 1
+LAG_Z = 2
+LAG_U = 3
+LAG_OUT = 4
+
+FLOPS = 2 * 2 * B * D * D
+
+
+def quantise_weight(nc, const, psum, ident, raw, label, bank_tag):
+    raw_words = raw[:].bitcast(F32)
+    grouped = const.tile([P, SLOTS * D], BF16, name=label + "_grouped", align_bytes=64)
+    grouped_words = grouped[:].bitcast(F32)
+    for pair in range(2):
+        bank = psum.tile([P, D], F32, name=label + "_bank", tag=bank_tag)
+        for c in range(2):
+            for h in range(2):
+                first = (2 * pair + c) * WORDS + h * P
+                nc.tensor.transpose(
+                    bank[:, (2 * c + h) * P : (2 * c + h + 1) * P],
+                    raw_words[:, first : first + P],
+                    ident[:],
+                )
+        nc.vector.tensor_copy(
+            out=grouped_words[:, pair * D : (pair + 1) * D].rearrange(
+                "p (c m h) -> p c m h", c=2, h=2
+            ),
+            in_=bank[:].rearrange("p (c h m) -> p c m h", c=2, h=2),
+        )
+    codes = const.tile([P, D], U32, name=label + "_codes", align_bytes=64)
+    scales = const.tile([P, D], U8, name=label + "_scales", align_bytes=64)
+    nc.vector.quantize_mx(out=codes[:].bitcast(FP8X4), scales=scales[:], in_=grouped[:])
+    return codes, scales
+
+
+def by_column(flat):
+    return flat.rearrange("p (c s) -> p c s", s=SLOTS)
+
+
+def bank_by_column(bank):
+    return bank.rearrange("p (s c) -> p c s", s=SLOTS)
+
+
+def pairs_by_column(flat):
+    return flat.rearrange("p (c h e) -> p c h e", h=2, e=2)
+
+
+def word_bank_by_column(bank):
+    return bank.bitcast(BF16).rearrange("p (h c e) -> p c h e", h=2, e=2)
+
+
+def tile_inimnetdisc_pa_t_kernel(tc, x, phi_j, phi_k, w_i, w_j, out):
+    nc = tc.nc
+    x_rows = x.rearrange("(p n) d -> p n d", n=N_BLOCKS)
+    j_rows = phi_j.rearrange("(p n) d -> p n d", n=N_BLOCKS)
+    k_rows = phi_k.rearrange("(p n) d -> p n d", n=N_BLOCKS)
+    out_rows = out.rearrange("(p n) d -> p n d", n=N_BLOCKS)
+
+    with ExitStack() as ctx:
+        ctx.enter_context(tc.manual_schedule())
+        const = ctx.enter_context(tc.tile_pool(name="const", bufs=1))
+        loads = ctx.enter_context(tc.tile_pool(name="loads", bufs=LOAD_AHEAD + 1))
+        work = ctx.enter_context(tc.tile_pool(name="work", bufs=2))
+        longer = ctx.enter_context(tc.tile_pool(name="longer", bufs=3))
+        psum_step = ctx.enter_context(tc.psum_pool(name="psum_step", bufs=1))
+        psum_block = ctx.enter_context(tc.psum_pool(name="psum_block", bufs=STEP_BLOCKS))
+
+        ident = const.tile([P, P], F32, name="ident")
+        make_identity(nc, ident[:])
+
+        x_in, k_in, j_in, pj, xT, kT, pjT, th, d1 = {}, {}, {}, {}, {}, {}, {}, {}, {}
+        r, g_mx, vT, z, u, u_mx, o_ps, weights = {}, {}, {}, {}, {}, {}, {}, {}
+
+        def load(s):
+            for rows, tiles, label in (
+                (k_rows, k_in, "k_in"),
+                (j_rows, j_in, "j_in"),
+                (x_rows, x_in, "x_in"),
+            ):
+                tiles[s] = loads.tile([P, STEP_BLOCKS * D], BF16, name=label)
+                nc.sync.dma_start(
+                    out=tiles[s][:].rearrange("p (n d) -> p n d", n=STEP_BLOCKS),
+                    in_=rows[:, s * STEP_BLOCKS : (s + 1) * STEP_BLOCKS, :],
+                )
+
+        def multiply_fields(s):
+            pj[s] = work.tile([P, STEP_ELEMS], F32, name="pj")
+            nc.gpsimd.tensor_tensor(
+                out=pj[s][:].rearrange("p (g e q) -> p g e q", e=2, q=P),
+                in0=k_in[s][:].rearrange("p (g q e) -> p g e q", e=2, q=P),
+                in1=j_in[s][:].rearrange("p (g q e) -> p g e q", e=2, q=P),
+                op=ALU.mult,
+            )
+
+        def transpose_words(src, dst):
+            src_words = src[:].bitcast(F32)
+            for blk in range(STEP_BLOCKS):
+                for h in range(2):
+                    first = blk * WORDS + h * P
+                    nc.tensor.transpose(
+                        dst[:, h * STEP_COLS + blk * P : h * STEP_COLS + (blk + 1) * P],
+                        src_words[:, first : first + P],
+                        ident[:],
+                    )
+
+        def transpose_x(s):
+            xT[s] = psum_step.tile([P, D], F32, name="xT")
+            transpose_words(x_in[s], xT[s])
+
+        def transpose_k(s):
+            kT[s] = psum_step.tile([P, D], F32, name="kT")
+            transpose_words(k_in[s], kT[s])
+
+        def transpose_pj(s):
+            pjT[s] = []
+            for blk in range(STEP_BLOCKS):
+                bank = psum_block.tile([P, BLOCK_ELEMS], F32, name="pjT")
+                for slot in range(SLOTS):
+                    first = (blk * SLOTS + slot) * P
+                    nc.tensor.transpose(
+                        bank[:, slot * P : (slot + 1) * P], pj[s][:, first : first + P], ident[:]
+                    )
+                pjT[s].append(bank)
+
+        def tanh(s):
+            th[s] = work.tile([P, STEP_ELEMS], F32, name="th")
+            nc.scalar.activation(
+                out=pairs_by_column(th[s][:]), in_=word_bank_by_column(xT[s][:]), func=ACT.Tanh
+            )
+
+        def tanh_derivative(s):
+            tt = work.tile([P, STEP_ELEMS], F32, name="tt")
+            nc.scalar.activation(out=tt[:], in_=th[s][:], func=ACT.Square)
+            d1[s] = longer.tile([P, STEP_ELEMS], F32, name="d1")
+            nc.scalar.activation(out=d1[s][:], in_=tt[:], func=ACT.Copy, scale=-1.0, bias=1.0)
+
+        def make_r(s):
+            r[s] = longer.tile([P, STEP_ELEMS], F32, name="r")
+            for blk in range(STEP_BLOCKS):
+                cols = slice(blk * BLOCK_ELEMS, (blk + 1) * BLOCK_ELEMS)
+                nc.vector.scalar_tensor_tensor(
+                    out=by_column(r[s][:, cols]),
+                    in0=by_column(th[s][:, cols]),
+                    scalar=-2.0,
+                    in1=bank_by_column(pjT[s][blk][:]),
+                    op0=ALU.mult,
+                    op1=ALU.mult,
+                )
+
+        def make_g(s):
+            g = work.tile([P, STEP_ELEMS], BF16, name="g", align_bytes=64)
+            nc.vector.tensor_tensor(
+                out=pairs_by_column(g[:]),
+                in0=pairs_by_column(d1[s][:]),
+                in1=word_bank_by_column(kT[s][:]),
+                op=ALU.mult,
+            )
+            return g
+
+        def quantise(values, label):
+            codes = work.tile([P, STEP_COLS], U32, name=label + "_codes", align_bytes=64)
+            scales = work.tile([P, STEP_COLS], U8, name=label + "_scales", align_bytes=64)
+            nc.vector.quantize_mx(out=codes[:].bitcast(FP8X4), scales=scales[:], in_=values[:])
+            return codes, scales
+
+        def first_matmul(s):
+            wj_codes, wj_scales = weights["wj"]
+            g_codes, g_scales = g_mx[s]
+            vT[s] = []
+            for blk in range(STEP_BLOCKS):
+                bank = psum_block.tile([P, BLOCK_ELEMS], F32, name="vT")
+                for slot in range(SLOTS):
+                    nc.tensor.matmul_mx(
+                        out=bank[:, slot * P : (slot + 1) * P],
+                        lhsT=wj_codes[:, slot * P : (slot + 1) * P].bitcast(FP8X4),
+                        lhsT_scale=wj_scales[:, slot * P : (slot + 1) * P],
+                        rhs=g_codes[:, blk * P : (blk + 1) * P].bitcast(FP8X4),
+                        rhs_scale=g_scales[:, blk * P : (blk + 1) * P],
+                        start=True,
+                        stop=True,
+                    )
+                vT[s].append(bank)
+
+        def make_z(s):
+            z[s] = work.tile([P, STEP_ELEMS], F32, name="z")
+            for blk in range(STEP_BLOCKS):
+                cols = slice(blk * BLOCK_ELEMS, (blk + 1) * BLOCK_ELEMS)
+                nc.vector.tensor_tensor(
+                    out=by_column(z[s][:, cols]),
+                    in0=by_column(r[s][:, cols]),
+                    in1=bank_by_column(vT[s][blk][:]),
+                    op=ALU.add,
+                )
+
+        def make_u(s):
+            u[s] = work.tile([P, STEP_ELEMS], BF16, name="u", align_bytes=64)
+            nc.gpsimd.tensor_tensor(out=u[s][:], in0=d1[s][:], in1=z[s][:], op=ALU.mult)
+
+        def second_matmul(s):
+            wi_codes, wi_scales = weights["wi"]
+            u_codes, u_scales = u_mx[s]
+            o_ps[s] = []
+            for blk in range(STEP_BLOCKS):
+                bank = psum_block.tile([P, D], F32, name="o_ps")
+                nc.tensor.matmul_mx(
+                    out=bank[:],
+                    lhsT=u_codes[:, blk * P : (blk + 1) * P].bitcast(FP8X4),
+                    lhsT_scale=u_scales[:, blk * P : (blk + 1) * P],
+                    rhs=wi_codes[:].bitcast(FP8X4),
+                    rhs_scale=wi_scales[:],
+                    start=True,
+                    stop=True,
+                )
+                o_ps[s].append(bank)
+
+        def store(s):
+            out_sb = longer.tile([P, STEP_BLOCKS * D], F32, name="out_sb")
+            for blk in range(STEP_BLOCKS):
+                nc.scalar.copy(out=out_sb[:, blk * D : (blk + 1) * D], in_=o_ps[s][blk][:])
+            nc.scalar.dma_start(
+                out=out_rows[:, s * STEP_BLOCKS : (s + 1) * STEP_BLOCKS, :],
+                in_=out_sb[:].rearrange("p (n d) -> p n d", n=STEP_BLOCKS),
+            )
+
+        load(0)
+        wj_raw = const.tile([P, SLOTS * D], BF16, name="wj_raw")
+        nc.sync.dma_start(
+            out=wj_raw[:].rearrange("m (h e k) -> m h e k", h=2, e=2),
+            in_=w_j.rearrange("(h m e) k -> m h e k", h=2, e=2),
+        )
+        wi_raw = const.tile([P, SLOTS * D], BF16, name="wi_raw")
+        nc.sync.dma_start(
+            out=wi_raw[:].rearrange("m (c k) -> m c k", c=4),
+            in_=w_i.rearrange("(c m) k -> m c k", c=4),
+        )
+        for s in range(1, LOAD_AHEAD):
+            load(s)
+
+        def live(s):
+            return 0 <= s < N_STEPS
+
+        for i in range(N_STEPS + LAG_OUT):
+            if live(i + LOAD_AHEAD):
+                load(i + LOAD_AHEAD)
+            if i == LAG_G:
+                weights["wj"] = quantise_weight(nc, const, psum_block, ident, wj_raw, "wj", "vT")
+            if i == LAG_U:
+                weights["wi"] = quantise_weight(nc, const, psum_block, ident, wi_raw, "wi", "o_ps")
+
+            if live(i):
+                multiply_fields(i)
+            if live(i - LAG_U):
+                make_u(i - LAG_U)
+            if live(i):
+                transpose_x(i)
+            if live(i - LAG_G):
+                make_r(i - LAG_G)
+            if live(i):
+                transpose_pj(i)
+            if live(i - LAG_G):
+                tanh_derivative(i - LAG_G)
+            if live(i - LAG_OUT):
+                store(i - LAG_OUT)
+            if live(i):
+                tanh(i)
+            if live(i - LAG_G):
+                g = make_g(i - LAG_G)
+            if live(i):
+                transpose_k(i)
+            if live(i - LAG_Z):
+                make_z(i - LAG_Z)
+            if live(i - LAG_G):
+                g_mx[i - LAG_G] = quantise(g, "g")
+            if live(i - LAG_U):
+                u_mx[i - LAG_U] = quantise(u[i - LAG_U], "u")
+            if live(i - LAG_G):
+                first_matmul(i - LAG_G)
+            if live(i - LAG_U):
+                second_matmul(i - LAG_U)

@@ -108,13 +108,8 @@ def tile_inimnetdisc_pa_t_kernel(tc, x, phi_j, phi_k, w_i, w_j, out):
                 )
 
         def multiply_fields(s):
-            pj[s] = work.tile([P, STEP_ELEMS], F32, name="pj")
-            nc.gpsimd.tensor_tensor(
-                out=pj[s][:].rearrange("p (g e q) -> p g e q", e=2, q=P),
-                in0=k_in[s][:].rearrange("p (g q e) -> p g e q", e=2, q=P),
-                in1=j_in[s][:].rearrange("p (g q e) -> p g e q", e=2, q=P),
-                op=ALU.mult,
-            )
+            pj[s] = work.tile([P, STEP_BLOCKS * D], F32, name="pj")
+            nc.gpsimd.tensor_tensor(out=pj[s][:], in0=k_in[s][:], in1=j_in[s][:], op=ALU.mult)
 
         def transpose_words(src, dst):
             src_words = src[:].bitcast(F32)
@@ -136,13 +131,15 @@ def tile_inimnetdisc_pa_t_kernel(tc, x, phi_j, phi_k, w_i, w_j, out):
             transpose_words(k_in[s], kT[s])
 
         def transpose_pj(s):
+            by_slot = pj[s][:].rearrange("p (b h q e) -> p b h e q", b=STEP_BLOCKS, h=2, e=2)
             pjT[s] = []
             for blk in range(STEP_BLOCKS):
                 bank = psum_block.tile([P, BLOCK_ELEMS], F32, name="pjT")
                 for slot in range(SLOTS):
-                    first = (blk * SLOTS + slot) * P
                     nc.tensor.transpose(
-                        bank[:, slot * P : (slot + 1) * P], pj[s][:, first : first + P], ident[:]
+                        bank[:, slot * P : (slot + 1) * P],
+                        by_slot[:, blk, slot // 2, slot % 2, :],
+                        ident[:],
                     )
                 pjT[s].append(bank)
 

@@ -15,7 +15,9 @@ P = 128
 B = 4096
 D = 512
 SLOTS = 4
+HALVES = 2
 WORDS = D // 2
+CHUNKS = D // P
 N_BLOCKS = B // P
 STEP_BLOCKS = 2
 N_STEPS = N_BLOCKS // STEP_BLOCKS
@@ -24,7 +26,7 @@ STEP_ELEMS = STEP_COLS * SLOTS
 BLOCK_ELEMS = P * SLOTS
 LOAD_AHEAD = 4
 LAG_G = 1
-LAG_Z = 2
+LAG_V = 2
 LAG_U = 3
 LAG_OUT = 4
 
@@ -33,23 +35,24 @@ FLOPS = 2 * 2 * B * D * D
 
 def quantise_weight(nc, const, psum, ident, raw, label, bank_tag):
     raw_words = raw[:].bitcast(F32)
-    grouped = const.tile([P, SLOTS * D], BF16, name=label + "_grouped", align_bytes=64)
+    grouped = const.tile([P, CHUNKS * P * SLOTS], BF16, name=label + "_grouped", align_bytes=64)
     grouped_words = grouped[:].bitcast(F32)
-    for pair in range(2):
+    chunks_a_bank = D // (HALVES * P)
+    for first_chunk in range(0, CHUNKS, chunks_a_bank):
         bank = psum.tile([P, D], F32, name=label + "_bank", tag=bank_tag)
-        for c in range(2):
-            for h in range(2):
-                first = (2 * pair + c) * WORDS + h * P
+        for a in range(chunks_a_bank):
+            for h in range(HALVES):
+                first = (first_chunk + a) * WORDS + h * P
                 nc.tensor.transpose(
-                    bank[:, (2 * c + h) * P : (2 * c + h + 1) * P],
+                    bank[:, (HALVES * a + h) * P : (HALVES * a + h + 1) * P],
                     raw_words[:, first : first + P],
                     ident[:],
                 )
-        nc.vector.tensor_copy(
-            out=grouped_words[:, pair * D : (pair + 1) * D].rearrange(
-                "p (c m h) -> p c m h", c=2, h=2
+        nc.scalar.copy(
+            out=grouped_words[:, first_chunk * WORDS : (first_chunk + chunks_a_bank) * WORDS].rearrange(
+                "p (a m h) -> p a m h", a=chunks_a_bank, h=HALVES
             ),
-            in_=bank[:].rearrange("p (c h m) -> p c m h", c=2, h=2),
+            in_=bank[:].rearrange("p (a h m) -> p a m h", a=chunks_a_bank, h=HALVES),
         )
     codes = const.tile([P, D], U32, name=label + "_codes", align_bytes=64)
     scales = const.tile([P, D], U8, name=label + "_scales", align_bytes=64)
@@ -58,19 +61,19 @@ def quantise_weight(nc, const, psum, ident, raw, label, bank_tag):
 
 
 def by_column(flat):
-    return flat.rearrange("p (c s) -> p c s", s=SLOTS)
+    return flat.rearrange("p (c t) -> p c t", t=SLOTS)
 
 
 def bank_by_column(bank):
-    return bank.rearrange("p (s c) -> p c s", s=SLOTS)
+    return bank.rearrange("p (t c) -> p c t", t=SLOTS)
 
 
 def pairs_by_column(flat):
-    return flat.rearrange("p (c h e) -> p c h e", h=2, e=2)
+    return flat.rearrange("p (c h e) -> p c h e", h=HALVES, e=2)
 
 
 def word_bank_by_column(bank):
-    return bank.bitcast(BF16).rearrange("p (h c e) -> p c h e", h=2, e=2)
+    return bank.bitcast(BF16).rearrange("p (h c e) -> p c h e", h=HALVES, e=2)
 
 
 def tile_inimnetdisc_pa_t_kernel(tc, x, phi_j, phi_k, w_i, w_j, out):
@@ -85,21 +88,21 @@ def tile_inimnetdisc_pa_t_kernel(tc, x, phi_j, phi_k, w_i, w_j, out):
         const = ctx.enter_context(tc.tile_pool(name="const", bufs=1))
         loads = ctx.enter_context(tc.tile_pool(name="loads", bufs=LOAD_AHEAD + 1))
         work = ctx.enter_context(tc.tile_pool(name="work", bufs=2))
-        longer = ctx.enter_context(tc.tile_pool(name="longer", bufs=3))
+        longer = ctx.enter_context(tc.tile_pool(name="longer", bufs=LAG_U + 1))
         psum_step = ctx.enter_context(tc.psum_pool(name="psum_step", bufs=1))
         psum_block = ctx.enter_context(tc.psum_pool(name="psum_block", bufs=STEP_BLOCKS))
 
         ident = const.tile([P, P], F32, name="ident")
         make_identity(nc, ident[:])
 
-        x_in, k_in, j_in, pj, xT, kT, pjT, th, d1 = {}, {}, {}, {}, {}, {}, {}, {}, {}
-        r, g_mx, vT, z, u, u_mx, o_ps, weights = {}, {}, {}, {}, {}, {}, {}, {}
+        x_in, k_in, j_in, xT, kT, jT, th, tt, d1, tj = {}, {}, {}, {}, {}, {}, {}, {}, {}, {}
+        tjk, vT, z, o_ps, weights, ug, codes, scales = {}, {}, {}, {}, {}, {}, {}, {}
 
         def load(s):
             for rows, tiles, label in (
-                (k_rows, k_in, "k_in"),
-                (j_rows, j_in, "j_in"),
                 (x_rows, x_in, "x_in"),
+                (j_rows, j_in, "j_in"),
+                (k_rows, k_in, "k_in"),
             ):
                 tiles[s] = loads.tile([P, STEP_BLOCKS * D], BF16, name=label)
                 nc.sync.dma_start(
@@ -107,14 +110,10 @@ def tile_inimnetdisc_pa_t_kernel(tc, x, phi_j, phi_k, w_i, w_j, out):
                     in_=rows[:, s * STEP_BLOCKS : (s + 1) * STEP_BLOCKS, :],
                 )
 
-        def multiply_fields(s):
-            pj[s] = work.tile([P, STEP_BLOCKS * D], F32, name="pj")
-            nc.gpsimd.tensor_tensor(out=pj[s][:], in0=k_in[s][:], in1=j_in[s][:], op=ALU.mult)
-
         def transpose_words(src, dst):
             src_words = src[:].bitcast(F32)
             for blk in range(STEP_BLOCKS):
-                for h in range(2):
+                for h in range(HALVES):
                     first = blk * WORDS + h * P
                     nc.tensor.transpose(
                         dst[:, h * STEP_COLS + blk * P : h * STEP_COLS + (blk + 1) * P],
@@ -126,22 +125,13 @@ def tile_inimnetdisc_pa_t_kernel(tc, x, phi_j, phi_k, w_i, w_j, out):
             xT[s] = psum_step.tile([P, D], F32, name="xT")
             transpose_words(x_in[s], xT[s])
 
-        def transpose_k(s):
-            kT[s] = psum_step.tile([P, D], F32, name="kT")
-            transpose_words(k_in[s], kT[s])
+        def transpose_j(s):
+            jT[s] = psum_step.tile([P, D], F32, name="jT")
+            transpose_words(j_in[s], jT[s])
 
-        def transpose_pj(s):
-            by_slot = pj[s][:].rearrange("p (b h q e) -> p b h e q", b=STEP_BLOCKS, h=2, e=2)
-            pjT[s] = []
-            for blk in range(STEP_BLOCKS):
-                bank = psum_block.tile([P, BLOCK_ELEMS], F32, name="pjT")
-                for slot in range(SLOTS):
-                    nc.tensor.transpose(
-                        bank[:, slot * P : (slot + 1) * P],
-                        by_slot[:, blk, slot // 2, slot % 2, :],
-                        ident[:],
-                    )
-                pjT[s].append(bank)
+        def transpose_k(s):
+            kT[s] = psum_step.tile([P, D], F32, name="kT", bufs=2)
+            transpose_words(k_in[s], kT[s])
 
         def tanh(s):
             th[s] = work.tile([P, STEP_ELEMS], F32, name="th")
@@ -149,54 +139,72 @@ def tile_inimnetdisc_pa_t_kernel(tc, x, phi_j, phi_k, w_i, w_j, out):
                 out=pairs_by_column(th[s][:]), in_=word_bank_by_column(xT[s][:]), func=ACT.Tanh
             )
 
-        def tanh_derivative(s):
-            tt = work.tile([P, STEP_ELEMS], F32, name="tt")
-            nc.scalar.activation(out=tt[:], in_=th[s][:], func=ACT.Square)
-            d1[s] = longer.tile([P, STEP_ELEMS], F32, name="d1")
-            nc.scalar.activation(out=d1[s][:], in_=tt[:], func=ACT.Copy, scale=-1.0, bias=1.0)
+        def square(s):
+            tt[s] = work.tile([P, STEP_ELEMS], F32, name="tt")
+            nc.scalar.activation(out=tt[s][:], in_=th[s][:], func=ACT.Square)
 
-        def make_r(s):
-            r[s] = longer.tile([P, STEP_ELEMS], F32, name="r")
-            for blk in range(STEP_BLOCKS):
-                cols = slice(blk * BLOCK_ELEMS, (blk + 1) * BLOCK_ELEMS)
-                nc.vector.scalar_tensor_tensor(
-                    out=by_column(r[s][:, cols]),
-                    in0=by_column(th[s][:, cols]),
-                    scalar=-2.0,
-                    in1=bank_by_column(pjT[s][blk][:]),
-                    op0=ALU.mult,
-                    op1=ALU.mult,
-                )
+        def one_minus_square(s):
+            d1[s] = longer.tile([P, STEP_ELEMS], F32, name="d1")
+            nc.scalar.activation(out=d1[s][:], in_=tt[s][:], func=ACT.Copy, scale=-1.0, bias=1.0)
+
+        def make_tj(s):
+            tj[s] = work.tile([P, STEP_ELEMS], F32, name="tj")
+            nc.vector.tensor_tensor(
+                out=pairs_by_column(tj[s][:]),
+                in0=pairs_by_column(th[s][:]),
+                in1=word_bank_by_column(jT[s][:]),
+                op=ALU.mult,
+            )
+
+        def make_tjk(s):
+            tjk[s] = longer.tile([P, STEP_ELEMS], F32, name="tjk")
+            nc.vector.tensor_tensor(
+                out=pairs_by_column(tjk[s][:]),
+                in0=pairs_by_column(tj[s][:]),
+                in1=word_bank_by_column(kT[s][:]),
+                op=ALU.mult,
+            )
+
+        def tiles_to_quantise(n):
+            ug[n] = work.tile([P, 2 * STEP_ELEMS], BF16, name="ug", align_bytes=64)
+            codes[n] = work.tile([P, 2 * STEP_COLS], U32, name="codes", align_bytes=64)
+            scales[n] = work.tile([P, 2 * STEP_COLS], U8, name="scales", align_bytes=64)
 
         def make_g(s):
-            g = work.tile([P, STEP_ELEMS], BF16, name="g", align_bytes=64)
             nc.vector.tensor_tensor(
-                out=pairs_by_column(g[:]),
+                out=pairs_by_column(ug[s + LAG_G][:, STEP_ELEMS:]),
                 in0=pairs_by_column(d1[s][:]),
                 in1=word_bank_by_column(kT[s][:]),
                 op=ALU.mult,
             )
-            return g
 
-        def quantise(values, label):
-            codes = work.tile([P, STEP_COLS], U32, name=label + "_codes", align_bytes=64)
-            scales = work.tile([P, STEP_COLS], U8, name=label + "_scales", align_bytes=64)
-            nc.vector.quantize_mx(out=codes[:].bitcast(FP8X4), scales=scales[:], in_=values[:])
-            return codes, scales
+        def make_u(s):
+            nc.gpsimd.tensor_tensor(
+                out=ug[s + LAG_U][:, :STEP_ELEMS], in0=d1[s][:], in1=z[s][:], op=ALU.mult
+            )
+
+        def quantise(n):
+            first = 0 if live(n - LAG_U) else STEP_COLS
+            last = 2 * STEP_COLS if live(n - LAG_G) else STEP_COLS
+            nc.vector.quantize_mx(
+                out=codes[n][:, first:last].bitcast(FP8X4),
+                scales=scales[n][:, first:last],
+                in_=ug[n][:, first * SLOTS : last * SLOTS],
+            )
 
         def first_matmul(s):
             wj_codes, wj_scales = weights["wj"]
-            g_codes, g_scales = g_mx[s]
             vT[s] = []
             for blk in range(STEP_BLOCKS):
+                cols = slice(STEP_COLS + blk * P, STEP_COLS + (blk + 1) * P)
                 bank = psum_block.tile([P, BLOCK_ELEMS], F32, name="vT")
                 for slot in range(SLOTS):
                     nc.tensor.matmul_mx(
                         out=bank[:, slot * P : (slot + 1) * P],
                         lhsT=wj_codes[:, slot * P : (slot + 1) * P].bitcast(FP8X4),
                         lhsT_scale=wj_scales[:, slot * P : (slot + 1) * P],
-                        rhs=g_codes[:, blk * P : (blk + 1) * P].bitcast(FP8X4),
-                        rhs_scale=g_scales[:, blk * P : (blk + 1) * P],
+                        rhs=codes[s + LAG_G][:, cols].bitcast(FP8X4),
+                        rhs_scale=scales[s + LAG_G][:, cols],
                         start=True,
                         stop=True,
                     )
@@ -206,27 +214,25 @@ def tile_inimnetdisc_pa_t_kernel(tc, x, phi_j, phi_k, w_i, w_j, out):
             z[s] = work.tile([P, STEP_ELEMS], F32, name="z")
             for blk in range(STEP_BLOCKS):
                 cols = slice(blk * BLOCK_ELEMS, (blk + 1) * BLOCK_ELEMS)
-                nc.vector.tensor_tensor(
+                nc.vector.scalar_tensor_tensor(
                     out=by_column(z[s][:, cols]),
-                    in0=by_column(r[s][:, cols]),
+                    in0=by_column(tjk[s][:, cols]),
+                    scalar=-2.0,
                     in1=bank_by_column(vT[s][blk][:]),
-                    op=ALU.add,
+                    op0=ALU.mult,
+                    op1=ALU.add,
                 )
-
-        def make_u(s):
-            u[s] = work.tile([P, STEP_ELEMS], BF16, name="u", align_bytes=64)
-            nc.gpsimd.tensor_tensor(out=u[s][:], in0=d1[s][:], in1=z[s][:], op=ALU.mult)
 
         def second_matmul(s):
             wi_codes, wi_scales = weights["wi"]
-            u_codes, u_scales = u_mx[s]
             o_ps[s] = []
             for blk in range(STEP_BLOCKS):
+                cols = slice(blk * P, (blk + 1) * P)
                 bank = psum_block.tile([P, D], F32, name="o_ps")
                 nc.tensor.matmul_mx(
                     out=bank[:],
-                    lhsT=u_codes[:, blk * P : (blk + 1) * P].bitcast(FP8X4),
-                    lhsT_scale=u_scales[:, blk * P : (blk + 1) * P],
+                    lhsT=codes[s + LAG_U][:, cols].bitcast(FP8X4),
+                    lhsT_scale=scales[s + LAG_U][:, cols],
                     rhs=wi_codes[:].bitcast(FP8X4),
                     rhs_scale=wi_scales[:],
                     start=True,
@@ -234,67 +240,66 @@ def tile_inimnetdisc_pa_t_kernel(tc, x, phi_j, phi_k, w_i, w_j, out):
                 )
                 o_ps[s].append(bank)
 
-        def store(s):
-            out_sb = longer.tile([P, STEP_BLOCKS * D], F32, name="out_sb")
-            for blk in range(STEP_BLOCKS):
-                nc.scalar.copy(out=out_sb[:, blk * D : (blk + 1) * D], in_=o_ps[s][blk][:])
-            nc.scalar.dma_start(
-                out=out_rows[:, s * STEP_BLOCKS : (s + 1) * STEP_BLOCKS, :],
-                in_=out_sb[:].rearrange("p (n d) -> p n d", n=STEP_BLOCKS),
-            )
+        def store(s, blk):
+            out_sb = longer.tile([P, D], F32, name="out_sb", bufs=2 * STEP_BLOCKS)
+            nc.scalar.copy(out=out_sb[:], in_=o_ps[s][blk][:])
+            nc.sync.dma_start(out=out_rows[:, s * STEP_BLOCKS + blk, :], in_=out_sb[:])
 
         load(0)
-        wj_raw = const.tile([P, SLOTS * D], BF16, name="wj_raw")
+        wj_raw = const.tile([P, CHUNKS * D], BF16, name="wj_raw")
         nc.sync.dma_start(
-            out=wj_raw[:].rearrange("m (h e k) -> m h e k", h=2, e=2),
-            in_=w_j.rearrange("(h m e) k -> m h e k", h=2, e=2),
+            out=wj_raw[:].rearrange("m (h e k) -> m h e k", h=HALVES, e=2),
+            in_=w_j.rearrange("(h m e) k -> m h e k", h=HALVES, e=2),
         )
-        wi_raw = const.tile([P, SLOTS * D], BF16, name="wi_raw")
+        load(1)
+        wi_raw = const.tile([P, CHUNKS * D], BF16, name="wi_raw")
         nc.sync.dma_start(
-            out=wi_raw[:].rearrange("m (c k) -> m c k", c=4),
-            in_=w_i.rearrange("(c m) k -> m c k", c=4),
+            out=wi_raw[:].rearrange("m (a k) -> m a k", a=CHUNKS),
+            in_=w_i.rearrange("(a m) k -> m a k", a=CHUNKS),
         )
-        for s in range(1, LOAD_AHEAD):
+        for s in range(2, LOAD_AHEAD):
             load(s)
 
         def live(s):
             return 0 <= s < N_STEPS
 
-        for i in range(N_STEPS + LAG_OUT):
-            if live(i + LOAD_AHEAD):
-                load(i + LOAD_AHEAD)
-            if i == LAG_G:
-                weights["wj"] = quantise_weight(nc, const, psum_block, ident, wj_raw, "wj", "vT")
-            if i == LAG_U:
-                weights["wi"] = quantise_weight(nc, const, psum_block, ident, wi_raw, "wi", "o_ps")
+        transpose_x(0)
+        for n in range(N_STEPS + LAG_OUT):
+            if live(n + LOAD_AHEAD):
+                load(n + LOAD_AHEAD)
+            if live(n - LAG_U) or live(n - LAG_G):
+                tiles_to_quantise(n)
 
-            if live(i):
-                multiply_fields(i)
-            if live(i - LAG_U):
-                make_u(i - LAG_U)
-            if live(i):
-                transpose_x(i)
-            if live(i - LAG_G):
-                make_r(i - LAG_G)
-            if live(i):
-                transpose_pj(i)
-            if live(i - LAG_G):
-                tanh_derivative(i - LAG_G)
-            if live(i - LAG_OUT):
-                store(i - LAG_OUT)
-            if live(i):
-                tanh(i)
-            if live(i - LAG_G):
-                g = make_g(i - LAG_G)
-            if live(i):
-                transpose_k(i)
-            if live(i - LAG_Z):
-                make_z(i - LAG_Z)
-            if live(i - LAG_G):
-                g_mx[i - LAG_G] = quantise(g, "g")
-            if live(i - LAG_U):
-                u_mx[i - LAG_U] = quantise(u[i - LAG_U], "u")
-            if live(i - LAG_G):
-                first_matmul(i - LAG_G)
-            if live(i - LAG_U):
-                second_matmul(i - LAG_U)
+            if live(n - LAG_OUT):
+                second_matmul(n - LAG_OUT)
+            if live(n - LAG_U):
+                make_z(n - LAG_U)
+                make_u(n - LAG_U)
+            if live(n - LAG_V):
+                first_matmul(n - LAG_V)
+            if live(n):
+                tanh(n)
+            if live(n - LAG_OUT):
+                store(n - LAG_OUT, 0)
+            if live(n):
+                square(n)
+            if live(n - LAG_OUT):
+                store(n - LAG_OUT, 1)
+            if live(n):
+                one_minus_square(n)
+            if live(n - LAG_G):
+                make_tj(n - LAG_G)
+                make_g(n - LAG_G)
+                make_tjk(n - LAG_G)
+            if live(n):
+                transpose_j(n)
+                transpose_k(n)
+            if live(n + 1):
+                transpose_x(n + 1)
+            if live(n - LAG_U) or live(n - LAG_G):
+                quantise(n)
+
+            if n == LAG_V - 1:
+                weights["wj"] = quantise_weight(nc, const, psum_block, ident, wj_raw, "wj", "vT")
+            if n == LAG_OUT - 1:
+                weights["wi"] = quantise_weight(nc, const, psum_block, ident, wi_raw, "wi", "o_ps")

from contextlib import ExitStack

import concourse.mybir as mybir
from concourse.masks import make_identity

F32 = mybir.dt.float32
BF16 = mybir.dt.bfloat16
U32 = mybir.dt.uint32
U8 = mybir.dt.uint8
FP8X4 = mybir.dt.float8_e4m3fn_x4
ACT = mybir.ActivationFunctionType
ALU = mybir.AluOpType

P = 128
B = 4096
D = 512
SLOTS = 4
HALVES = 2
WORDS = D // 2
CHUNKS = D // P
N_BLOCKS = B // P
STEP_BLOCKS = 2
N_STEPS = N_BLOCKS // STEP_BLOCKS
STEP_COLS = STEP_BLOCKS * P
STEP_ELEMS = STEP_COLS * SLOTS
BLOCK_ELEMS = P * SLOTS
LOAD_AHEAD = 4
LAG_G = 1
LAG_V = 2
LAG_U = 3
LAG_OUT = 4

FLOPS = 2 * 2 * B * D * D


def quantise_weight(nc, const, psum, ident, raw, label, bank_tag):
    raw_words = raw[:].bitcast(F32)
    grouped = const.tile([P, CHUNKS * P * SLOTS], BF16, name=label + "_grouped", align_bytes=64)
    grouped_words = grouped[:].bitcast(F32)
    chunks_a_bank = D // (HALVES * P)
    for first_chunk in range(0, CHUNKS, chunks_a_bank):
        bank = psum.tile([P, D], F32, name=label + "_bank", tag=bank_tag)
        for a in range(chunks_a_bank):
            for h in range(HALVES):
                first = (first_chunk + a) * WORDS + h * P
                nc.tensor.transpose(
                    bank[:, (HALVES * a + h) * P : (HALVES * a + h + 1) * P],
                    raw_words[:, first : first + P],
                    ident[:],
                )
        nc.scalar.copy(
            out=grouped_words[:, first_chunk * WORDS : (first_chunk + chunks_a_bank) * WORDS].rearrange(
                "p (a m h) -> p a m h", a=chunks_a_bank, h=HALVES
            ),
            in_=bank[:].rearrange("p (a h m) -> p a m h", a=chunks_a_bank, h=HALVES),
        )
    codes = const.tile([P, D], U32, name=label + "_codes", align_bytes=64)
    scales = const.tile([P, D], U8, name=label + "_scales", align_bytes=64)
    nc.vector.quantize_mx(out=codes[:].bitcast(FP8X4), scales=scales[:], in_=grouped[:])
    return codes, scales


def by_column(flat):
    return flat.rearrange("p (c t) -> p c t", t=SLOTS)


def bank_by_column(bank):
    return bank.rearrange("p (t c) -> p c t", t=SLOTS)


def pairs_by_column(flat):
    return flat.rearrange("p (c h e) -> p c h e", h=HALVES, e=2)


def word_bank_by_column(bank):
    return bank.bitcast(BF16).rearrange("p (h c e) -> p c h e", h=HALVES, e=2)


def tile_inimnetdisc_pa_t_kernel(tc, x, phi_j, phi_k, w_i, w_j, out):
    nc = tc.nc
    x_rows = x.rearrange("(p n) d -> p n d", n=N_BLOCKS)
    j_rows = phi_j.rearrange("(p n) d -> p n d", n=N_BLOCKS)
    k_rows = phi_k.rearrange("(p n) d -> p n d", n=N_BLOCKS)
    out_rows = out.rearrange("(p n) d -> p n d", n=N_BLOCKS)

    with ExitStack() as ctx:
        ctx.enter_context(tc.manual_schedule())
        const = ctx.enter_context(tc.tile_pool(name="const", bufs=1))
        loads = ctx.enter_context(tc.tile_pool(name="loads", bufs=LOAD_AHEAD + 1))
        work = ctx.enter_context(tc.tile_pool(name="work", bufs=2))
        longer = ctx.enter_context(tc.tile_pool(name="longer", bufs=LAG_U + 1))
        psum_step = ctx.enter_context(tc.psum_pool(name="psum_step", bufs=1))
        psum_block = ctx.enter_context(tc.psum_pool(name="psum_block", bufs=STEP_BLOCKS))

        ident = const.tile([P, P], F32, name="ident")
        make_identity(nc, ident[:])

        x_in, k_in, j_in, xT, kT, jT, th, tt, d1, tj = {}, {}, {}, {}, {}, {}, {}, {}, {}, {}
        tjk, vT, z, o_ps, weights, ug, codes, scales = {}, {}, {}, {}, {}, {}, {}, {}

        def load(s):
            for rows, tiles, label in (
                (x_rows, x_in, "x_in"),
                (j_rows, j_in, "j_in"),
                (k_rows, k_in, "k_in"),
            ):
                tiles[s] = loads.tile([P, STEP_BLOCKS * D], BF16, name=label)
                nc.sync.dma_start(
                    out=tiles[s][:].rearrange("p (n d) -> p n d", n=STEP_BLOCKS),
                    in_=rows[:, s * STEP_BLOCKS : (s + 1) * STEP_BLOCKS, :],
                )

        def transpose_words(src, dst):
            src_words = src[:].bitcast(F32)
            for blk in range(STEP_BLOCKS):
                for h in range(HALVES):
                    first = blk * WORDS + h * P
                    nc.tensor.transpose(
                        dst[:, h * STEP_COLS + blk * P : h * STEP_COLS + (blk + 1) * P],
                        src_words[:, first : first + P],
                        ident[:],
                    )

        def transpose_x(s):
            xT[s] = psum_step.tile([P, D], F32, name="xT")
            transpose_words(x_in[s], xT[s])

        def transpose_j(s):
            jT[s] = psum_step.tile([P, D], F32, name="jT")
            transpose_words(j_in[s], jT[s])

        def transpose_k(s):
            kT[s] = psum_step.tile([P, D], F32, name="kT", bufs=2)
            transpose_words(k_in[s], kT[s])

        def tanh(s):
            th[s] = work.tile([P, STEP_ELEMS], F32, name="th")
            nc.scalar.activation(
                out=pairs_by_column(th[s][:]), in_=word_bank_by_column(xT[s][:]), func=ACT.Tanh
            )

        def square(s):
            tt[s] = work.tile([P, STEP_ELEMS], F32, name="tt")
            nc.scalar.activation(out=tt[s][:], in_=th[s][:], func=ACT.Square)

        def one_minus_square(s):
            d1[s] = longer.tile([P, STEP_ELEMS], F32, name="d1")
            nc.scalar.activation(out=d1[s][:], in_=tt[s][:], func=ACT.Copy, scale=-1.0, bias=1.0)

        def make_tj(s):
            tj[s] = work.tile([P, STEP_ELEMS], F32, name="tj")
            nc.vector.tensor_tensor(
                out=pairs_by_column(tj[s][:]),
                in0=pairs_by_column(th[s][:]),
                in1=word_bank_by_column(jT[s][:]),
                op=ALU.mult,
            )

        def make_tjk(s):
            tjk[s] = longer.tile([P, STEP_ELEMS], F32, name="tjk")
            nc.vector.tensor_tensor(
                out=pairs_by_column(tjk[s][:]),
                in0=pairs_by_column(tj[s][:]),
                in1=word_bank_by_column(kT[s][:]),
                op=ALU.mult,
            )

        def tiles_to_quantise(n):
            ug[n] = work.tile([P, 2 * STEP_ELEMS], BF16, name="ug", align_bytes=64)
            codes[n] = work.tile([P, 2 * STEP_COLS], U32, name="codes", align_bytes=64)
            scales[n] = work.tile([P, 2 * STEP_COLS], U8, name="scales", align_bytes=64)

        def make_g(s):
            nc.vector.tensor_tensor(
                out=pairs_by_column(ug[s + LAG_G][:, STEP_ELEMS:]),
                in0=pairs_by_column(d1[s][:]),
                in1=word_bank_by_column(kT[s][:]),
                op=ALU.mult,
            )

        def make_u(s):
            nc.gpsimd.tensor_tensor(
                out=ug[s + LAG_U][:, :STEP_ELEMS], in0=d1[s][:], in1=z[s][:], op=ALU.mult
            )

        def quantise(n):
            first = 0 if live(n - LAG_U) else STEP_COLS
            last = 2 * STEP_COLS if live(n - LAG_G) else STEP_COLS
            nc.vector.quantize_mx(
                out=codes[n][:, first:last].bitcast(FP8X4),
                scales=scales[n][:, first:last],
                in_=ug[n][:, first * SLOTS : last * SLOTS],
            )

        def first_matmul(s):
            wj_codes, wj_scales = weights["wj"]
            vT[s] = []
            for blk in range(STEP_BLOCKS):
                cols = slice(STEP_COLS + blk * P, STEP_COLS + (blk + 1) * P)
                bank = psum_block.tile([P, BLOCK_ELEMS], F32, name="vT")
                for slot in range(SLOTS):
                    nc.tensor.matmul_mx(
                        out=bank[:, slot * P : (slot + 1) * P],
                        lhsT=wj_codes[:, slot * P : (slot + 1) * P].bitcast(FP8X4),
                        lhsT_scale=wj_scales[:, slot * P : (slot + 1) * P],
                        rhs=codes[s + LAG_G][:, cols].bitcast(FP8X4),
                        rhs_scale=scales[s + LAG_G][:, cols],
                        start=True,
                        stop=True,
                    )
                vT[s].append(bank)

        def make_z(s):
            z[s] = work.tile([P, STEP_ELEMS], F32, name="z")
            for blk in range(STEP_BLOCKS):
                cols = slice(blk * BLOCK_ELEMS, (blk + 1) * BLOCK_ELEMS)
                nc.vector.scalar_tensor_tensor(
                    out=by_column(z[s][:, cols]),
                    in0=by_column(tjk[s][:, cols]),
                    scalar=-2.0,
                    in1=bank_by_column(vT[s][blk][:]),
                    op0=ALU.mult,
                    op1=ALU.add,
                )

        def second_matmul(s):
            wi_codes, wi_scales = weights["wi"]
            o_ps[s] = []
            for blk in range(STEP_BLOCKS):
                cols = slice(blk * P, (blk + 1) * P)
                bank = psum_block.tile([P, D], F32, name="o_ps")
                nc.tensor.matmul_mx(
                    out=bank[:],
                    lhsT=codes[s + LAG_U][:, cols].bitcast(FP8X4),
                    lhsT_scale=scales[s + LAG_U][:, cols],
                    rhs=wi_codes[:].bitcast(FP8X4),
                    rhs_scale=wi_scales[:],
                    start=True,
                    stop=True,
                )
                o_ps[s].append(bank)

        def store(s, blk):
            out_sb = longer.tile([P, D], F32, name="out_sb", bufs=2 * STEP_BLOCKS)
            nc.scalar.copy(out=out_sb[:], in_=o_ps[s][blk][:])
            nc.sync.dma_start(out=out_rows[:, s * STEP_BLOCKS + blk, :], in_=out_sb[:])

        load(0)
        wj_raw = const.tile([P, CHUNKS * D], BF16, name="wj_raw")
        nc.sync.dma_start(
            out=wj_raw[:].rearrange("m (h e k) -> m h e k", h=HALVES, e=2),
            in_=w_j.rearrange("(h m e) k -> m h e k", h=HALVES, e=2),
        )
        load(1)
        wi_raw = const.tile([P, CHUNKS * D], BF16, name="wi_raw")
        nc.sync.dma_start(
            out=wi_raw[:].rearrange("m (a k) -> m a k", a=CHUNKS),
            in_=w_i.rearrange("(a m) k -> m a k", a=CHUNKS),
        )
        for s in range(2, LOAD_AHEAD):
            load(s)

        def live(s):
            return 0 <= s < N_STEPS

        transpose_x(0)
        for n in range(N_STEPS + LAG_OUT):
            if live(n + LOAD_AHEAD):
                load(n + LOAD_AHEAD)
            if live(n - LAG_U) or live(n - LAG_G):
                tiles_to_quantise(n)

            if live(n - LAG_OUT):
                second_matmul(n - LAG_OUT)
            if live(n - LAG_U):
                make_z(n - LAG_U)
                make_u(n - LAG_U)
            if live(n - LAG_V):
                first_matmul(n - LAG_V)
            if live(n):
                tanh(n)
            if live(n - LAG_OUT):
                store(n - LAG_OUT, 0)
            if live(n):
                square(n)
            if live(n - LAG_OUT):
                store(n - LAG_OUT, 1)
            if live(n):
                one_minus_square(n)
            if live(n - LAG_G):
                make_tj(n - LAG_G)
                make_g(n - LAG_G)
                make_tjk(n - LAG_G)
            if live(n):
                transpose_j(n)
                transpose_k(n)
            if live(n + 1):
                transpose_x(n + 1)
            if live(n - LAG_U) or live(n - LAG_G):
                quantise(n)

            if n == LAG_V - 1:
                weights["wj"] = quantise_weight(nc, const, psum_block, ident, wj_raw, "wj", "vT")
            if n == LAG_OUT - 1:
                weights["wi"] = quantise_weight(nc, const, psum_block, ident, wi_raw, "wi", "o_ps")
